import numpy as np
import ml_dtypes


def mxq(x, axis, fmt="e4m3"):
    dtype, down = {"e4m3": (ml_dtypes.float8_e4m3fn, 7), "e5m2": (ml_dtypes.float8_e5m2, 14)}[fmt]
    v = np.moveaxis(np.asarray(x, np.float32).astype(ml_dtypes.bfloat16).astype(np.float64), axis, -1)
    blocks = v.reshape(v.shape[:-1] + (-1, 32))
    amax = np.abs(blocks).max(-1, keepdims=True)
    byte = np.maximum(np.where(amax > 0, np.frexp(amax)[1] - 1 + 127, 0) - down, 1)
    scale = np.exp2(byte - 127.0)
    codes = (blocks / scale).astype(np.float32).astype(dtype).astype(np.float64)
    return np.moveaxis((codes * scale).reshape(v.shape), -1, axis)


WIDE = False


def mx_kscale(k):
    if not WIDE:
        return np.ones(k)
    levels = np.array([10, -10, 5, -5, 0])
    if k % 512:
        return np.exp2(np.random.permutation(np.resize(levels, k // 32))).repeat(32)
    a = np.empty((k // 512, 16))
    for p in range(k // 512):
        a[p, :8] = np.random.permutation(np.resize(levels, 8))
        for g in range(8):
            far = levels[np.abs(levels - a[p, g]) >= 10]
            a[p, g + 8] = far[np.random.randint(len(far))]
    return np.exp2(a.ravel()).repeat(32)


BF16 = ml_dtypes.bfloat16


def bf(x):
    return np.asarray(x, np.float32).astype(BF16)


def f64(x):
    return np.asarray(x).astype(np.float64)


B, T, G, I, H = 4, 1024, 4, 512, 128


def setup_inputs():
    s = mx_kscale(I)
    return {"x": bf((np.random.standard_normal((B, T, G, I)) * s).reshape(B, T, G * I)),
            "W": bf(np.random.standard_normal((G, H, I)) / np.sqrt(I) / s),
            "b": bf(np.random.standard_normal((G, H)) * 0.5)}


def reference(x, W, b):
    xg = f64(x).reshape(B, T, G, I)
    xq = mxq(xg, 3, "e4m3")
    wq = mxq(f64(W), 2, "e4m3")
    y = xq.transpose(2, 0, 1, 3).reshape(G, B * T, I) @ wq.transpose(0, 2, 1)
    out = y.reshape(G, B, T, H).transpose(1, 2, 0, 3) + f64(b)
    return np.swapaxes(out, -1, -2).reshape(B, T, G * H)

from contextlib import ExitStack

import concourse.mybir as mybir
from concourse.masks import make_identity

F32 = mybir.dt.float32
BF16 = mybir.dt.bfloat16
U32 = mybir.dt.uint32
U8 = mybir.dt.uint8
FP8X4 = mybir.dt.float8_e4m3fn_x4
ADD = mybir.AluOpType.add

P = 128
G = 4
I = 512
H = 128
TOKENS = 4096
NT = TOKENS // P
FEAT = G * I
WORDS = FEAT // 2
BANK = 512
FLOPS = 2 * TOKENS * G * I * H

LOAD_TILES = [1, 1, 2, 4, 4, 4, 4, 4, 8]
STORE_TILES = [16, 8, 4, 2, 1, 1]
UNIT = 2


def tile_groupedlinear_t_kernel(tc, x, W, b, out):
    nc = tc.nc
    x_rows = x.flatten_outer_dims().rearrange("(p j) f -> p j f", j=NT)
    out_rows = out.flatten_outer_dims().rearrange("(p j) c -> p j c", j=NT)

    with ExitStack() as ctx:
        const = ctx.enter_context(tc.tile_pool(name="const", bufs=1))
        xpool = ctx.enter_context(tc.tile_pool(name="xpool", bufs=1))
        opool = ctx.enter_context(tc.tile_pool(name="opool", bufs=1))
        gpool = ctx.enter_context(tc.tile_pool(name="gpool", bufs=4))
        qpool = ctx.enter_context(tc.tile_pool(name="qpool", bufs=4))
        tpool = ctx.enter_context(tc.psum_pool(name="tpool", bufs=6))
        apool = ctx.enter_context(tc.psum_pool(name="apool", bufs=2))
        ctx.enter_context(tc.manual_schedule())

        brow = const.tile([P, G * H], BF16)
        nc.vector.memset(brow[:], 0.0)
        ones = const.tile([P, P], BF16)
        nc.vector.memset(ones[:], 1.0)
        ident = const.tile([P, P], F32)
        make_identity(nc, ident[:])

        nc.scalar.dma_start(out=brow[0:1, :], in_=b.rearrange("(o g) h -> o (g h)", o=1))
        w_sb = const.tile([P, FEAT], BF16)
        nc.sync.dma_start(
            out=w_sb[:].rearrange("p (g i) -> p g i", g=G), in_=W.rearrange("g h i -> h g i")
        )
        x_words = []
        j0 = 0
        for n, cnt in enumerate(LOAD_TILES):
            piece = xpool.tile([P, cnt, FEAT], BF16, name="x%d" % n)
            nc.sync.dma_start(out=piece[:], in_=x_rows[:, j0 : j0 + cnt, :])
            for jj in range(cnt):
                x_words.append(piece[:, jj, :].bitcast(F32))
            j0 += cnt

        out_slots = []
        j0 = 0
        for n, cnt in enumerate(STORE_TILES):
            opiece = opool.tile([P, cnt, G * H], F32, name="o%d" % n)
            for jj in range(cnt):
                out_slots.append((opiece, jj, j0, cnt))
            j0 += cnt

        def transpose_and_group(words):
            grouped = gpool.tile([P, FEAT], BF16, align_bytes=64)
            gw = grouped[:].bitcast(F32)
            for half in range(2):
                bank = tpool.tile([P, BANK], F32)
                for q in range(4):
                    col = BANK * half + 2 * P * (q // 2) + q % 2
                    nc.tensor.transpose(
                        bank[:, P * q : P * (q + 1)],
                        words[:, col : col + 2 * P - 1 : 2],
                        ident[:],
                    )
                nc.scalar.copy(
                    out=gw[:, BANK * half : BANK * (half + 1)].rearrange(
                        "p (g r u) -> p g r u", g=2, u=2
                    ),
                    in_=bank[:].rearrange("p (g u r) -> p g r u", g=2, u=2),
                )
            return grouped

        def quantise(grouped, codes, scales):
            nc.vector.quantize_mx(out=codes[:].bitcast(FP8X4), scales=scales[:], in_=grouped[:])

        w_codes = const.tile([P, G * H], U32, align_bytes=64)
        w_scales = const.tile([P, G * H], U8, align_bytes=64)
        quantise(transpose_and_group(w_sb[:].bitcast(F32)), w_codes, w_scales)

        bias_ps = apool.tile([P, BANK], F32, tag="acc")
        nc.tensor.matmul(bias_ps[:], lhsT=ones[:], rhs=brow[:], start=True, stop=True)
        bias_sb = const.tile([P, G * H], F32)
        nc.vector.tensor_copy(
            out=bias_sb[:].rearrange("p (h g) -> p h g", g=G),
            in_=bias_ps[:].rearrange("p (g h) -> p h g", g=G),
        )

        def multiply(codes, scales):
            acc = apool.tile([P, BANK], F32, tag="acc")
            for g in range(G):
                cols = slice(H * g, H * (g + 1))
                nc.tensor.matmul_mx(
                    out=acc[:, cols],
                    lhsT=codes[:, cols].bitcast(FP8X4),
                    lhsT_scale=scales[:, cols],
                    rhs=w_codes[:, cols].bitcast(FP8X4),
                    rhs_scale=w_scales[:, cols],
                    start=True,
                    stop=True,
                )
            return acc

        def finish(j, acc):
            opiece, jj, first, cnt = out_slots[j]
            nc.vector.tensor_tensor(
                out=opiece[:, jj, :].rearrange("p (h g) -> p h g", g=G),
                in0=acc[:].rearrange("p (g h) -> p h g", g=G),
                in1=bias_sb[:].rearrange("p (h g) -> p h g", g=G),
                op=ADD,
            )
            if jj == cnt - 1:
                nc.sync.dma_start(out=out_rows[:, first : first + cnt, :], in_=opiece[:])

        units = NT // UNIT
        quantised = {}
        for u in range(units + 1):
            grouped = {}
            accs = {}
            if u < units:
                for j in range(UNIT * u, UNIT * (u + 1)):
                    grouped[j] = transpose_and_group(x_words[j])
            if u >= 1:
                for j in range(UNIT * (u - 1), UNIT * u):
                    accs[j] = multiply(quantised[j][0], quantised[j][1])
            for k in range(UNIT):
                if u < units:
                    j = UNIT * u + k
                    codes = qpool.tile([P, G * P], U32, align_bytes=64)
                    scales = qpool.tile([P, G * P], U8, align_bytes=64)
                    quantise(grouped[j], codes, scales)
                    quantised[j] = (codes, scales)
                if u >= 1:
                    j = UNIT * (u - 1) + k
                    finish(j, accs[j])
